import numpy as np
import ml_dtypes


def mxq(x, axis, fmt="e4m3"):
    dtype, down = {"e4m3": (ml_dtypes.float8_e4m3fn, 7), "e5m2": (ml_dtypes.float8_e5m2, 14)}[fmt]
    v = np.moveaxis(np.asarray(x, np.float32).astype(ml_dtypes.bfloat16).astype(np.float64), axis, -1)
    blocks = v.reshape(v.shape[:-1] + (-1, 32))
    amax = np.abs(blocks).max(-1, keepdims=True)
    byte = np.maximum(np.where(amax > 0, np.frexp(amax)[1] - 1 + 127, 0) - down, 1)
    scale = np.exp2(byte - 127.0)
    codes = (blocks / scale).astype(np.float32).astype(dtype).astype(np.float64)
    return np.moveaxis((codes * scale).reshape(v.shape), -1, axis)


WIDE = False


def mx_kscale(k):
    if not WIDE:
        return np.ones(k)
    levels = np.array([10, -10, 5, -5, 0])
    if k % 512:
        return np.exp2(np.random.permutation(np.resize(levels, k // 32))).repeat(32)
    a = np.empty((k // 512, 16))
    for p in range(k // 512):
        a[p, :8] = np.random.permutation(np.resize(levels, 8))
        for g in range(8):
            far = levels[np.abs(levels - a[p, g]) >= 10]
            a[p, g + 8] = far[np.random.randint(len(far))]
    return np.exp2(a.ravel()).repeat(32)


BF16 = ml_dtypes.bfloat16


def bf(x):
    return np.asarray(x, np.float32).astype(BF16)


def f64(x):
    return np.asarray(x).astype(np.float64)


BATCH, IN_F, OUT_F, RANK, N_ADAPTERS = 1024, 2048, 2048, 128, 8
SEG = BATCH // N_ADAPTERS
LORA_GAIN = 2.0


def setup_inputs():
    s = mx_kscale(IN_F)
    return {"x": bf(np.random.standard_normal((BATCH, IN_F)) * s),
            "h_lora": bf(np.random.standard_normal((N_ADAPTERS, SEG, RANK))),
            "lora_B": bf(np.random.standard_normal((N_ADAPTERS, RANK, OUT_F)) * 0.5 / np.sqrt(RANK)),
            "M": bf(np.random.standard_normal((IN_F, OUT_F)) / np.sqrt(IN_F) / s[:, None])}


def core(x, h_lora, lora_B, M):
    y = (f64(h_lora) @ f64(lora_B)) * LORA_GAIN
    y = y.reshape(BATCH, OUT_F)
    return y + (mxq(f64(x), 1, "e4m3") @ mxq(f64(M), 0, "e4m3"))


def e4m3fn_bytes(y):
    return np.clip(np.asarray(y, np.float64), -448.0, 448.0).astype(np.float32).astype(ml_dtypes.float8_e4m3fn).view(np.uint8)


Y_SCALE = 150.0


def reference(x, h_lora, lora_B, M):
    out = core(x, h_lora, lora_B, M)
    return out, e4m3fn_bytes(out * Y_SCALE)

@@ -1,0 +1,247 @@
+from contextlib import ExitStack
+
+import concourse.mybir as mybir
+from concourse.masks import make_identity
+
+ROWS, K, N, RANK, SEGS = 1024, 2048, 2048, 128, 8
+FLOPS = 2 * ROWS * K * N + 2 * ROWS * RANK * N
+
+F32 = mybir.dt.float32
+BF16 = mybir.dt.bfloat16
+U32 = mybir.dt.uint32
+U8 = mybir.dt.uint8
+FP8X4 = mybir.dt.float8_e4m3fn_x4
+FP8 = mybir.dt.float8_e4m3fn
+COPY = mybir.ActivationFunctionType.Copy
+ADD = mybir.AluOpType.add
+MULT = mybir.AluOpType.mult
+
+P = 128
+PACK = 4
+K_PASS = P * PACK
+PASSES = K // K_PASS
+NT = 512
+HALF = 2 * NT
+CHUNKS = N // NT
+LORA_GAIN = 2.0
+Y_SCALE = 150.0
+
+S_COLS = (128, 128, 128, 128)
+
+
+def tile_lorasequential_pa_kernel(tc, x, h_lora, lora_B, M, out_0, out_1):
+    nc = tc.nc
+    with ExitStack() as ctx:
+        keep = ctx.enter_context(tc.tile_pool(name="keep", bufs=1))
+        xraw_pool = ctx.enter_context(tc.tile_pool(name="xraw", bufs=4))
+        xgrp_pool = ctx.enter_context(tc.tile_pool(name="xgrp", bufs=2))
+        mraw_pool = ctx.enter_context(tc.tile_pool(name="mraw", bufs=8))
+        mwide_pool = ctx.enter_context(tc.tile_pool(name="mwide", bufs=4))
+        mgrp_pool = ctx.enter_context(tc.tile_pool(name="mgrp", bufs=3))
+        mq_pool = ctx.enter_context(tc.tile_pool(name="mq", bufs=10))
+        b_pool = ctx.enter_context(tc.tile_pool(name="bpool", bufs=2))
+        lo_pool = ctx.enter_context(tc.tile_pool(name="lo", bufs=4))
+        o_pool = ctx.enter_context(tc.tile_pool(name="o", bufs=8))
+        f8_pool = ctx.enter_context(tc.tile_pool(name="f8", bufs=8))
+        ps_mx = ctx.enter_context(tc.psum_pool(name="psmx", bufs=4))
+        ps_lo = ctx.enter_context(tc.psum_pool(name="pslo", bufs=2))
+        ps_tp = ctx.enter_context(tc.psum_pool(name="pstp", bufs=2))
+
+        ident_f = keep.tile([P, P], F32, name="ident_f", tag="ident_f")
+        make_identity(nc, ident_f[:])
+        ident_b = keep.tile([P, P], BF16, name="ident_b", tag="ident_b")
+        make_identity(nc, ident_b[:])
+        warm = keep.tile([P, 2], F32, name="warm", tag="warm")
+        nc.vector.memset(warm[:], 0.0)
+        nc.scalar.activation(out=warm[:, 1:2], in_=warm[:, 0:1], func=COPY, scale=1.0)
+
+        xc = keep.tile([P, SEGS * PASSES * P], U32, name="xc", tag="xc", align_bytes=64)
+        xs = keep.tile([P, SEGS * PASSES * P], U8, name="xs", tag="xs", align_bytes=64)
+        h_sb = keep.tile([P, SEGS, RANK], BF16, name="h_sb", tag="h_sb")
+        hT = keep.tile([P, SEGS * P], BF16, name="hT", tag="hT")
+
+        xraw = {}
+        mraw = {}
+        btile = {}
+        mq = {}
+        mgrp = {}
+
+        def load_x(m):
+            t = xraw_pool.tile([P, K], BF16, name="xraw", tag="xraw")
+            nc.sync.dma_start(out=t[:], in_=x[m * P:(m + 1) * P, :])
+            xraw[m] = t
+
+        def load_m(c, g):
+            t = mraw_pool.tile([P, PACK, NT], BF16, name="mraw", tag="mraw")
+            nc.sync.dma_start(
+                out=t[:],
+                in_=M[g * K_PASS:(g + 1) * K_PASS, c * NT:(c + 1) * NT].rearrange("(p j) w -> p j w", j=PACK),
+            )
+            mraw[(c, g)] = t[:]
+
+        def load_m_wide(half, g):
+            t = mwide_pool.tile([P, PACK, HALF], BF16, name="mwide", tag="mwide")
+            nc.sync.dma_start(
+                out=t[:],
+                in_=M[g * K_PASS:(g + 1) * K_PASS, half * HALF:(half + 1) * HALF].rearrange("(p j) w -> p j w", j=PACK),
+            )
+            mraw[(2 * half, g)] = t[:, :, 0:NT]
+            mraw[(2 * half + 1, g)] = t[:, :, NT:HALF]
+
+        def load_b(half, parts):
+            t = b_pool.tile([P, SEGS, HALF], BF16, name="btile", tag="btile")
+            step = SEGS // parts
+            btile[half] = t
+            return [(t, half, i * step, (i + 1) * step) for i in range(parts)]
+
+        def load_b_part(part):
+            t, half, g0, g1 = part
+            nc.sync.dma_start(
+                out=t[:, g0:g1, :],
+                in_=lora_B[g0:g1, :, half * HALF:(half + 1) * HALF].rearrange("g r n -> r g n"),
+            )
+
+        def load_h():
+            nc.sync.dma_start(out=h_sb[:], in_=h_lora.rearrange("g b r -> b g r"))
+
+        def prep_x(m):
+            words = xraw[m][:].bitcast(F32)
+            grp = xgrp_pool.tile([P, PASSES * P * PACK], BF16, name="xgrp", tag="xgrp", align_bytes=64)
+            gw = grp[:].bitcast(F32).rearrange("p (g r u) -> p g r u", g=PASSES, u=2)
+            for half in range(2):
+                tp = ps_tp.tile([P, 2, 2, P], F32, name="tp", tag="tp")
+                for gg in range(2):
+                    g = 2 * half + gg
+                    for u in range(2):
+                        nc.tensor.transpose(tp[:, gg, u, :], words[:, 256 * g + u:256 * (g + 1):2], ident_f[:])
+                nc.scalar.copy(out=gw[:, 2 * half:2 * half + 2, :, :], in_=tp[:].rearrange("p g u r -> p g r u"))
+            sl = slice(m * PASSES * P, (m + 1) * PASSES * P)
+            nc.vector.quantize_mx(out=xc[:, sl].bitcast(FP8X4), scales=xs[:, sl], in_=grp[:])
+
+        def prep_h():
+            tp = ps_tp.tile([P, SEGS, P], BF16, name="tp", tag="tp")
+            for g in range(SEGS):
+                nc.tensor.transpose(tp[:, g, :], h_sb[:, g, :], ident_b[:])
+            nc.vector.tensor_copy(out=hT[:], in_=tp[:].rearrange("p g b -> p (g b)"))
+
+        def unit_copy(c, g):
+            raw = mraw[(c, g)]
+            grp = mgrp_pool.tile([P, NT, PACK], BF16, name="mgrp", tag="mgrp", align_bytes=64)
+            a = NT - S_COLS[c]
+            nc.vector.tensor_copy(out=grp[:, 0:a, :], in_=raw[:, :, 0:a].rearrange("p j w -> p w j"))
+            if a < NT:
+                nc.scalar.copy(out=grp[:, a:NT, :], in_=raw[:, :, a:NT].rearrange("p j w -> p w j"))
+            mgrp[(c, g)] = grp
+
+        def unit_quant(c, g):
+            codes = mq_pool.tile([P, NT], U32, name="mcodes", tag="mcodes", align_bytes=64)
+            scales = mq_pool.tile([P, NT], U8, name="mscales", tag="mscales", align_bytes=64)
+            nc.vector.quantize_mx(
+                out=codes[:].bitcast(FP8X4), scales=scales[:], in_=mgrp[(c, g)][:].rearrange("p w j -> p (w j)")
+            )
+            mq[(c, g)] = (codes, scales)
+
+        lo_sb = {}
+        acc_ps = {}
+
+        def lora(m, c):
+            lp = ps_lo.tile([P, NT], F32, name="lp", tag="lp")
+            nc.tensor.matmul(out=lp[:], lhsT=hT[:, m * P:(m + 1) * P], rhs=btile[c // 2][:, m, (c % 2) * NT:(c % 2 + 1) * NT], start=True, stop=True)
+            lo = lo_pool.tile([P, NT], F32, name="lo", tag="lo")
+            nc.scalar.activation(out=lo[:], in_=lp[:], func=COPY, scale=LORA_GAIN)
+            lo_sb[(m, c)] = lo
+
+        def mx(m, c):
+            acc = ps_mx.tile([P, NT], F32, name="acc", tag="acc")
+            for g in range(PASSES):
+                codes, scales = mq[(c, g)]
+                sl = slice((m * PASSES + g) * P, (m * PASSES + g + 1) * P)
+                nc.tensor.matmul_mx(
+                    out=acc[:],
+                    lhsT=xc[:, sl].bitcast(FP8X4),
+                    lhsT_scale=xs[:, sl],
+                    rhs=codes[:].bitcast(FP8X4),
+                    rhs_scale=scales[:],
+                    start=(g == 0),
+                    stop=(g == PASSES - 1),
+                )
+            acc_ps[(m, c)] = acc
+
+        o_sb = {}
+        f8_sb = {}
+
+        def epilogue(m, c):
+            half = c // 2
+            if c % 2 == 0:
+                o_sb[(m, half)] = o_pool.tile([P, HALF], F32, name="o", tag="o")
+                f8_sb[(m, half)] = f8_pool.tile([P, HALF], FP8, name="f8", tag="f8")
+            o = o_sb[(m, half)]
+            f8 = f8_sb[(m, half)]
+            part = slice((c % 2) * NT, (c % 2 + 1) * NT)
+            nc.vector.tensor_tensor(out=o[:, part], in0=acc_ps[(m, c)][:], in1=lo_sb[(m, c)][:], op=ADD)
+            if c == CHUNKS - 1:
+                nc.vector.tensor_scalar(
+                    out=f8[:, part], in0=o[:, part], scalar1=Y_SCALE, scalar2=None, op0=MULT, saturate=False
+                )
+            else:
+                nc.scalar.activation(out=f8[:, part], in_=o[:, part], func=COPY, scale=Y_SCALE, saturate=False)
+            rows = slice(m * P, (m + 1) * P)
+            wide = slice(half * HALF, (half + 1) * HALF)
+            if half == 1:
+                nc.sync.dma_start(out=out_0[rows, c * NT:(c + 1) * NT], in_=o[:, part])
+            elif c % 2 == 1:
+                nc.sync.dma_start(out=out_0[rows, wide], in_=o[:])
+            if c % 2 == 1:
+                nc.sync.dma_start(out=out_1[rows, wide], in_=f8[:].bitcast(U8))
+
+        load_x(0)
+        load_x(1)
+        load_m(0, 0)
+        load_x(2)
+        load_m(0, 1)
+        load_x(3)
+        load_m(0, 2)
+        load_h()
+        load_m(0, 3)
+        b0 = load_b(0, 4)
+        load_b_part(b0[0])
+        load_x(4)
+        load_b_part(b0[1])
+        load_x(5)
+        load_x(6)
+        load_b_part(b0[2])
+        load_x(7)
+        load_b_part(b0[3])
+        for g in range(PASSES):
+            load_m(1, g)
+        for g in range(PASSES):
+            load_m_wide(1, g)
+        for part in load_b(1, 2):
+            load_b_part(part)
+
+        prep_x(0)
+        prep_x(1)
+        unit_copy(0, 0)
+        prep_x(2)
+        unit_quant(0, 0)
+        unit_copy(0, 1)
+        prep_x(3)
+        unit_quant(0, 1)
+        unit_copy(0, 2)
+        prep_h()
+        unit_quant(0, 2)
+        unit_copy(0, 3)
+        unit_quant(0, 3)
+
+        for c in range(CHUNKS):
+            for m in range(SEGS):
+                if c == 0 and m + 4 < SEGS:
+                    prep_x(m + 4)
+                lora(m, c)
+                mx(m, c)
+                if c + 1 < CHUNKS:
+                    if m % 2 == 0:
+                        unit_copy(c + 1, m // 2)
+                    else:
+                        unit_quant(c + 1, m // 2)
+                epilogue(m, c)

@@ -102,7 +102,7 @@ def tile_lorasequential_pa_kernel(tc, x, h_lora, lora_B, M, out_0, out_1):
             )
 
         def load_h():
-            nc.sync.dma_start(out=h_sb[:], in_=h_lora.rearrange("g b r -> b g r"))
+            nc.sync.dma_start(out=h_sb[:], in_=h_lora.rearrange("g b r -> (g b) r").rearrange("(p a) r -> p a r", a=SEGS))
 
         def prep_x(m):
             words = xraw[m][:].bitcast(F32)
@@ -120,17 +120,23 @@ def tile_lorasequential_pa_kernel(tc, x, h_lora, lora_B, M, out_0, out_1):
 
         def prep_h():
             tp = ps_tp.tile([P, SEGS, P], BF16, name="tp", tag="tp")
-            for g in range(SEGS):
-                nc.tensor.transpose(tp[:, g, :], h_sb[:, g, :], ident_b[:])
-            nc.vector.tensor_copy(out=hT[:], in_=tp[:].rearrange("p g b -> p (g b)"))
+            for a in range(SEGS):
+                nc.tensor.transpose(tp[:, a, :], h_sb[:, a, :], ident_b[:])
+            nc.vector.tensor_copy(out=hT[:].rearrange("r (p a) -> r p a", a=SEGS), in_=tp[:].rearrange("r a p -> r p a"))
 
         def unit_copy(c, g):
             raw = mraw[(c, g)]
             grp = mgrp_pool.tile([P, NT, PACK], BF16, name="mgrp", tag="mgrp", align_bytes=64)
             a = NT - S_COLS[c]
-            nc.vector.tensor_copy(out=grp[:, 0:a, :], in_=raw[:, :, 0:a].rearrange("p j w -> p w j"))
+            nc.vector.tensor_copy(
+                out=grp[:, 0:a, :].rearrange("p (c i) j -> p c j i", i=4),
+                in_=raw[:, :, 0:a].rearrange("p j (c i) -> p c j i", i=4),
+            )
             if a < NT:
-                nc.scalar.copy(out=grp[:, a:NT, :], in_=raw[:, :, a:NT].rearrange("p j w -> p w j"))
+                nc.scalar.copy(
+                    out=grp[:, a:NT, :].rearrange("p (c i) j -> p c j i", i=4),
+                    in_=raw[:, :, a:NT].rearrange("p j (c i) -> p c j i", i=4),
+                )
             mgrp[(c, g)] = grp
 
         def unit_quant(c, g):
@@ -180,10 +186,11 @@ def tile_lorasequential_pa_kernel(tc, x, h_lora, lora_B, M, out_0, out_1):
             part = slice((c % 2) * NT, (c % 2 + 1) * NT)
             nc.vector.tensor_tensor(out=o[:, part], in0=acc_ps[(m, c)][:], in1=lo_sb[(m, c)][:], op=ADD)
             if c == CHUNKS - 1:
+                nc.scalar.activation(out=f8[:, 0:NT], in_=o[:, 0:NT], func=COPY, scale=Y_SCALE, saturate=False)
                 nc.vector.tensor_scalar(
                     out=f8[:, part], in0=o[:, part], scalar1=Y_SCALE, scalar2=None, op0=MULT, saturate=False
                 )
-            else:
+            elif c != CHUNKS - 2:
                 nc.scalar.activation(out=f8[:, part], in_=o[:, part], func=COPY, scale=Y_SCALE, saturate=False)
             rows = slice(m * P, (m + 1) * P)
             wide = slice(half * HALF, (half + 1) * HALF)

@@ -26,23 +26,25 @@ CHUNKS = N // NT
 LORA_GAIN = 2.0
 Y_SCALE = 150.0
 
-S_COLS = (128, 128, 128, 128)
+S_COLS = 128
+RUN = 8
+X_AHEAD = 4
 
 
 def tile_lorasequential_pa_kernel(tc, x, h_lora, lora_B, M, out_0, out_1):
     nc = tc.nc
     with ExitStack() as ctx:
         keep = ctx.enter_context(tc.tile_pool(name="keep", bufs=1))
-        xraw_pool = ctx.enter_context(tc.tile_pool(name="xraw", bufs=4))
+        xraw_pool = ctx.enter_context(tc.tile_pool(name="xraw", bufs=X_AHEAD))
         xgrp_pool = ctx.enter_context(tc.tile_pool(name="xgrp", bufs=2))
-        mraw_pool = ctx.enter_context(tc.tile_pool(name="mraw", bufs=8))
-        mwide_pool = ctx.enter_context(tc.tile_pool(name="mwide", bufs=4))
+        mraw_pool = ctx.enter_context(tc.tile_pool(name="mraw", bufs=2 * PASSES))
+        mwide_pool = ctx.enter_context(tc.tile_pool(name="mwide", bufs=PASSES))
         mgrp_pool = ctx.enter_context(tc.tile_pool(name="mgrp", bufs=3))
-        mq_pool = ctx.enter_context(tc.tile_pool(name="mq", bufs=10))
+        mq_pool = ctx.enter_context(tc.tile_pool(name="mq", bufs=2 * PASSES + 2))
         b_pool = ctx.enter_context(tc.tile_pool(name="bpool", bufs=2))
         lo_pool = ctx.enter_context(tc.tile_pool(name="lo", bufs=4))
-        o_pool = ctx.enter_context(tc.tile_pool(name="o", bufs=8))
-        f8_pool = ctx.enter_context(tc.tile_pool(name="f8", bufs=8))
+        o_pool = ctx.enter_context(tc.tile_pool(name="o", bufs=SEGS))
+        f8_pool = ctx.enter_context(tc.tile_pool(name="f8", bufs=SEGS))
         ps_mx = ctx.enter_context(tc.psum_pool(name="psmx", bufs=4))
         ps_lo = ctx.enter_context(tc.psum_pool(name="pslo", bufs=2))
         ps_tp = ctx.enter_context(tc.psum_pool(name="pstp", bufs=2))
@@ -63,8 +65,12 @@ def tile_lorasequential_pa_kernel(tc, x, h_lora, lora_B, M, out_0, out_1):
         xraw = {}
         mraw = {}
         btile = {}
-        mq = {}
         mgrp = {}
+        mq = {}
+        lo_sb = {}
+        acc_ps = {}
+        o_sb = {}
+        f8_sb = {}
 
         def load_x(m):
             t = xraw_pool.tile([P, K], BF16, name="xraw", tag="xraw")
@@ -88,16 +94,12 @@ def tile_lorasequential_pa_kernel(tc, x, h_lora, lora_B, M, out_0, out_1):
             mraw[(2 * half, g)] = t[:, :, 0:NT]
             mraw[(2 * half + 1, g)] = t[:, :, NT:HALF]
 
-        def load_b(half, parts):
-            t = b_pool.tile([P, SEGS, HALF], BF16, name="btile", tag="btile")
-            step = SEGS // parts
-            btile[half] = t
-            return [(t, half, i * step, (i + 1) * step) for i in range(parts)]
+        def new_b(half):
+            btile[half] = b_pool.tile([P, SEGS, HALF], BF16, name="btile", tag="btile")
 
-        def load_b_part(part):
-            t, half, g0, g1 = part
+        def load_b(half, g0, g1):
             nc.sync.dma_start(
-                out=t[:, g0:g1, :],
+                out=btile[half][:, g0:g1, :],
                 in_=lora_B[g0:g1, :, half * HALF:(half + 1) * HALF].rearrange("g r n -> r g n"),
             )
 
@@ -108,13 +110,13 @@ def tile_lorasequential_pa_kernel(tc, x, h_lora, lora_B, M, out_0, out_1):
             words = xraw[m][:].bitcast(F32)
             grp = xgrp_pool.tile([P, PASSES * P * PACK], BF16, name="xgrp", tag="xgrp", align_bytes=64)
             gw = grp[:].bitcast(F32).rearrange("p (g r u) -> p g r u", g=PASSES, u=2)
-            for half in range(2):
+            for bank in range(2):
                 tp = ps_tp.tile([P, 2, 2, P], F32, name="tp", tag="tp")
                 for gg in range(2):
-                    g = 2 * half + gg
+                    g = 2 * bank + gg
                     for u in range(2):
                         nc.tensor.transpose(tp[:, gg, u, :], words[:, 256 * g + u:256 * (g + 1):2], ident_f[:])
-                nc.scalar.copy(out=gw[:, 2 * half:2 * half + 2, :, :], in_=tp[:].rearrange("p g u r -> p g r u"))
+                nc.scalar.copy(out=gw[:, 2 * bank:2 * bank + 2, :, :], in_=tp[:].rearrange("p g u r -> p g r u"))
             sl = slice(m * PASSES * P, (m + 1) * PASSES * P)
             nc.vector.quantize_mx(out=xc[:, sl].bitcast(FP8X4), scales=xs[:, sl], in_=grp[:])
 
@@ -127,16 +129,15 @@ def tile_lorasequential_pa_kernel(tc, x, h_lora, lora_B, M, out_0, out_1):
         def unit_copy(c, g):
             raw = mraw[(c, g)]
             grp = mgrp_pool.tile([P, NT, PACK], BF16, name="mgrp", tag="mgrp", align_bytes=64)
-            a = NT - S_COLS[c]
+            a = NT - S_COLS
             nc.vector.tensor_copy(
-                out=grp[:, 0:a, :].rearrange("p (c i) j -> p c j i", i=4),
-                in_=raw[:, :, 0:a].rearrange("p j (c i) -> p c j i", i=4),
+                out=grp[:, 0:a, :].rearrange("p (c i) j -> p c j i", i=RUN),
+                in_=raw[:, :, 0:a].rearrange("p j (c i) -> p c j i", i=RUN),
             )
-            if a < NT:
-                nc.scalar.copy(
-                    out=grp[:, a:NT, :].rearrange("p (c i) j -> p c j i", i=4),
-                    in_=raw[:, :, a:NT].rearrange("p j (c i) -> p c j i", i=4),
-                )
+            nc.scalar.copy(
+                out=grp[:, a:NT, :].rearrange("p (c i) j -> p c j i", i=RUN),
+                in_=raw[:, :, a:NT].rearrange("p j (c i) -> p c j i", i=RUN),
+            )
             mgrp[(c, g)] = grp
 
         def unit_quant(c, g):
@@ -146,9 +147,6 @@ def tile_lorasequential_pa_kernel(tc, x, h_lora, lora_B, M, out_0, out_1):
                 out=codes[:].bitcast(FP8X4), scales=scales[:], in_=mgrp[(c, g)][:].rearrange("p w j -> p (w j)")
             )
             mq[(c, g)] = (codes, scales)
-
-        lo_sb = {}
-        acc_ps = {}
 
         def lora(m, c):
             lp = ps_lo.tile([P, NT], F32, name="lp", tag="lp")
@@ -173,8 +171,22 @@ def tile_lorasequential_pa_kernel(tc, x, h_lora, lora_B, M, out_0, out_1):
                 )
             acc_ps[(m, c)] = acc
 
-        o_sb = {}
-        f8_sb = {}
+        def cast_scalar(m, c):
+            part = slice((c % 2) * NT, (c % 2 + 1) * NT)
+            nc.scalar.activation(
+                out=f8_sb[(m, c // 2)][:, part], in_=o_sb[(m, c // 2)][:, part], func=COPY, scale=Y_SCALE, saturate=False
+            )
+
+        def cast_vector(m, c):
+            part = slice((c % 2) * NT, (c % 2 + 1) * NT)
+            nc.vector.tensor_scalar(
+                out=f8_sb[(m, c // 2)][:, part],
+                in0=o_sb[(m, c // 2)][:, part],
+                scalar1=Y_SCALE,
+                scalar2=None,
+                op0=MULT,
+                saturate=False,
+            )
 
         def epilogue(m, c):
             half = c // 2
@@ -182,16 +194,13 @@ def tile_lorasequential_pa_kernel(tc, x, h_lora, lora_B, M, out_0, out_1):
                 o_sb[(m, half)] = o_pool.tile([P, HALF], F32, name="o", tag="o")
                 f8_sb[(m, half)] = f8_pool.tile([P, HALF], FP8, name="f8", tag="f8")
             o = o_sb[(m, half)]
-            f8 = f8_sb[(m, half)]
             part = slice((c % 2) * NT, (c % 2 + 1) * NT)
             nc.vector.tensor_tensor(out=o[:, part], in0=acc_ps[(m, c)][:], in1=lo_sb[(m, c)][:], op=ADD)
             if c == CHUNKS - 1:
-                nc.scalar.activation(out=f8[:, 0:NT], in_=o[:, 0:NT], func=COPY, scale=Y_SCALE, saturate=False)
-                nc.vector.tensor_scalar(
-                    out=f8[:, part], in0=o[:, part], scalar1=Y_SCALE, scalar2=None, op0=MULT, saturate=False
-                )
+                cast_scalar(m, c - 1)
+                cast_vector(m, c)
             elif c != CHUNKS - 2:
-                nc.scalar.activation(out=f8[:, part], in_=o[:, part], func=COPY, scale=Y_SCALE, saturate=False)
+                cast_scalar(m, c)
             rows = slice(m * P, (m + 1) * P)
             wide = slice(half * HALF, (half + 1) * HALF)
             if half == 1:
@@ -199,7 +208,7 @@ def tile_lorasequential_pa_kernel(tc, x, h_lora, lora_B, M, out_0, out_1):
             elif c % 2 == 1:
                 nc.sync.dma_start(out=out_0[rows, wide], in_=o[:])
             if c % 2 == 1:
-                nc.sync.dma_start(out=out_1[rows, wide], in_=f8[:].bitcast(U8))
+                nc.sync.dma_start(out=out_1[rows, wide], in_=f8_sb[(m, half)][:].bitcast(U8))
 
         load_x(0)
         load_x(1)
@@ -210,21 +219,22 @@ def tile_lorasequential_pa_kernel(tc, x, h_lora, lora_B, M, out_0, out_1):
         load_m(0, 2)
         load_h()
         load_m(0, 3)
-        b0 = load_b(0, 4)
-        load_b_part(b0[0])
+        new_b(0)
+        load_b(0, 0, 2)
         load_x(4)
-        load_b_part(b0[1])
+        load_b(0, 2, 4)
         load_x(5)
         load_x(6)
-        load_b_part(b0[2])
+        load_b(0, 4, 6)
         load_x(7)
-        load_b_part(b0[3])
+        load_b(0, 6, 8)
         for g in range(PASSES):
             load_m(1, g)
         for g in range(PASSES):
             load_m_wide(1, g)
-        for part in load_b(1, 2):
-            load_b_part(part)
+        new_b(1)
+        load_b(1, 0, 4)
+        load_b(1, 4, 8)
 
         prep_x(0)
         prep_x(1)
@@ -242,8 +252,8 @@ def tile_lorasequential_pa_kernel(tc, x, h_lora, lora_B, M, out_0, out_1):
 
         for c in range(CHUNKS):
             for m in range(SEGS):
-                if c == 0 and m + 4 < SEGS:
-                    prep_x(m + 4)
+                if c == 0 and m + X_AHEAD < SEGS:
+                    prep_x(m + X_AHEAD)
                 lora(m, c)
                 mx(m, c)
                 if c + 1 < CHUNKS:

@@ -20,6 +20,7 @@ P = 128
 PACK = 4
 K_PASS = P * PACK
 PASSES = K // K_PASS
+WORDS = K_PASS // 2
 NT = 512
 HALF = 2 * NT
 CHUNKS = N // NT
@@ -72,27 +73,27 @@ def tile_lorasequential_pa_kernel(tc, x, h_lora, lora_B, M, out_0, out_1):
         o_sb = {}
         f8_sb = {}
 
-        def load_x(m):
-            t = xraw_pool.tile([P, K], BF16, name="xraw", tag="xraw")
-            nc.sync.dma_start(out=t[:], in_=x[m * P:(m + 1) * P, :])
-            xraw[m] = t
+        def load_x(g):
+            tile_x = xraw_pool.tile([P, K], BF16, name="xraw", tag="xraw")
+            nc.sync.dma_start(out=tile_x[:], in_=x[g * P:(g + 1) * P, :])
+            xraw[g] = tile_x
 
-        def load_m(c, g):
-            t = mraw_pool.tile([P, PACK, NT], BF16, name="mraw", tag="mraw")
+        def load_m(c, s):
+            tile_m = mraw_pool.tile([P, PACK, NT], BF16, name="mraw", tag="mraw")
             nc.sync.dma_start(
-                out=t[:],
-                in_=M[g * K_PASS:(g + 1) * K_PASS, c * NT:(c + 1) * NT].rearrange("(p j) w -> p j w", j=PACK),
+                out=tile_m[:],
+                in_=M[s * K_PASS:(s + 1) * K_PASS, c * NT:(c + 1) * NT].rearrange("(p t) w -> p t w", t=PACK),
             )
-            mraw[(c, g)] = t[:]
+            mraw[(c, s)] = tile_m[:]
 
-        def load_m_wide(half, g):
-            t = mwide_pool.tile([P, PACK, HALF], BF16, name="mwide", tag="mwide")
+        def load_m_wide(half, s):
+            tile_m = mwide_pool.tile([P, PACK, HALF], BF16, name="mwide", tag="mwide")
             nc.sync.dma_start(
-                out=t[:],
-                in_=M[g * K_PASS:(g + 1) * K_PASS, half * HALF:(half + 1) * HALF].rearrange("(p j) w -> p j w", j=PACK),
+                out=tile_m[:],
+                in_=M[s * K_PASS:(s + 1) * K_PASS, half * HALF:(half + 1) * HALF].rearrange("(p t) w -> p t w", t=PACK),
             )
-            mraw[(2 * half, g)] = t[:, :, 0:NT]
-            mraw[(2 * half + 1, g)] = t[:, :, NT:HALF]
+            mraw[(2 * half, s)] = tile_m[:, :, 0:NT]
+            mraw[(2 * half + 1, s)] = tile_m[:, :, NT:HALF]
 
         def new_b(half):
             btile[half] = b_pool.tile([P, SEGS, HALF], BF16, name="btile", tag="btile")
@@ -100,25 +101,24 @@ def tile_lorasequential_pa_kernel(tc, x, h_lora, lora_B, M, out_0, out_1):
         def load_b(half, g0, g1):
             nc.sync.dma_start(
                 out=btile[half][:, g0:g1, :],
-                in_=lora_B[g0:g1, :, half * HALF:(half + 1) * HALF].rearrange("g r n -> r g n"),
+                in_=lora_B[g0:g1, :, half * HALF:(half + 1) * HALF].rearrange("g r w -> r g w"),
             )
 
         def load_h():
             nc.sync.dma_start(out=h_sb[:], in_=h_lora.rearrange("g b r -> (g b) r").rearrange("(p a) r -> p a r", a=SEGS))
 
-        def prep_x(m):
-            words = xraw[m][:].bitcast(F32)
+        def prep_x(g):
+            words = xraw[g][:].bitcast(F32)
             grp = xgrp_pool.tile([P, PASSES * P * PACK], BF16, name="xgrp", tag="xgrp", align_bytes=64)
-            gw = grp[:].bitcast(F32).rearrange("p (g r u) -> p g r u", g=PASSES, u=2)
-            for bank in range(2):
+            grp_words = grp[:].bitcast(F32).rearrange("p (s b u) -> p s b u", s=PASSES, u=2)
+            for bank in range(PASSES // 2):
                 tp = ps_tp.tile([P, 2, 2, P], F32, name="tp", tag="tp")
-                for gg in range(2):
-                    g = 2 * bank + gg
+                for s in (2 * bank, 2 * bank + 1):
                     for u in range(2):
-                        nc.tensor.transpose(tp[:, gg, u, :], words[:, 256 * g + u:256 * (g + 1):2], ident_f[:])
-                nc.scalar.copy(out=gw[:, 2 * bank:2 * bank + 2, :, :], in_=tp[:].rearrange("p g u r -> p g r u"))
-            sl = slice(m * PASSES * P, (m + 1) * PASSES * P)
-            nc.vector.quantize_mx(out=xc[:, sl].bitcast(FP8X4), scales=xs[:, sl], in_=grp[:])
+                        nc.tensor.transpose(tp[:, s % 2, u, :], words[:, WORDS * s + u:WORDS * (s + 1):2], ident_f[:])
+                nc.scalar.copy(out=grp_words[:, 2 * bank:2 * bank + 2, :, :], in_=tp[:].rearrange("p s u b -> p s b u"))
+            cols = slice(g * PASSES * P, (g + 1) * PASSES * P)
+            nc.vector.quantize_mx(out=xc[:, cols].bitcast(FP8X4), scales=xs[:, cols], in_=grp[:])
 
         def prep_h():
             tp = ps_tp.tile([P, SEGS, P], BF16, name="tp", tag="tp")
@@ -126,89 +126,89 @@ def tile_lorasequential_pa_kernel(tc, x, h_lora, lora_B, M, out_0, out_1):
                 nc.tensor.transpose(tp[:, a, :], h_sb[:, a, :], ident_b[:])
             nc.vector.tensor_copy(out=hT[:].rearrange("r (p a) -> r p a", a=SEGS), in_=tp[:].rearrange("r a p -> r p a"))
 
-        def unit_copy(c, g):
-            raw = mraw[(c, g)]
+        def unit_copy(c, s):
+            raw = mraw[(c, s)]
             grp = mgrp_pool.tile([P, NT, PACK], BF16, name="mgrp", tag="mgrp", align_bytes=64)
-            a = NT - S_COLS
+            v_cols = NT - S_COLS
             nc.vector.tensor_copy(
-                out=grp[:, 0:a, :].rearrange("p (c i) j -> p c j i", i=RUN),
-                in_=raw[:, :, 0:a].rearrange("p j (c i) -> p c j i", i=RUN),
+                out=grp[:, 0:v_cols, :].rearrange("p (n i) t -> p n t i", i=RUN),
+                in_=raw[:, :, 0:v_cols].rearrange("p t (n i) -> p n t i", i=RUN),
             )
             nc.scalar.copy(
-                out=grp[:, a:NT, :].rearrange("p (c i) j -> p c j i", i=RUN),
-                in_=raw[:, :, a:NT].rearrange("p j (c i) -> p c j i", i=RUN),
+                out=grp[:, v_cols:NT, :].rearrange("p (n i) t -> p n t i", i=RUN),
+                in_=raw[:, :, v_cols:NT].rearrange("p t (n i) -> p n t i", i=RUN),
             )
-            mgrp[(c, g)] = grp
+            mgrp[(c, s)] = grp
 
-        def unit_quant(c, g):
+        def unit_quant(c, s):
             codes = mq_pool.tile([P, NT], U32, name="mcodes", tag="mcodes", align_bytes=64)
             scales = mq_pool.tile([P, NT], U8, name="mscales", tag="mscales", align_bytes=64)
             nc.vector.quantize_mx(
-                out=codes[:].bitcast(FP8X4), scales=scales[:], in_=mgrp[(c, g)][:].rearrange("p w j -> p (w j)")
+                out=codes[:].bitcast(FP8X4), scales=scales[:], in_=mgrp[(c, s)][:].rearrange("p w t -> p (w t)")
             )
-            mq[(c, g)] = (codes, scales)
+            mq[(c, s)] = (codes, scales)
 
-        def lora(m, c):
+        def in_half(c):
+            return slice((c % 2) * NT, (c % 2 + 1) * NT)
+
+        def lora(g, c):
             lp = ps_lo.tile([P, NT], F32, name="lp", tag="lp")
-            nc.tensor.matmul(out=lp[:], lhsT=hT[:, m * P:(m + 1) * P], rhs=btile[c // 2][:, m, (c % 2) * NT:(c % 2 + 1) * NT], start=True, stop=True)
+            nc.tensor.matmul(out=lp[:], lhsT=hT[:, g * P:(g + 1) * P], rhs=btile[c // 2][:, g, in_half(c)], start=True, stop=True)
             lo = lo_pool.tile([P, NT], F32, name="lo", tag="lo")
             nc.scalar.activation(out=lo[:], in_=lp[:], func=COPY, scale=LORA_GAIN)
-            lo_sb[(m, c)] = lo
+            lo_sb[(g, c)] = lo
 
-        def mx(m, c):
+        def mx(g, c):
             acc = ps_mx.tile([P, NT], F32, name="acc", tag="acc")
-            for g in range(PASSES):
-                codes, scales = mq[(c, g)]
-                sl = slice((m * PASSES + g) * P, (m * PASSES + g + 1) * P)
+            for s in range(PASSES):
+                codes, scales = mq[(c, s)]
+                cols = slice((g * PASSES + s) * P, (g * PASSES + s + 1) * P)
                 nc.tensor.matmul_mx(
                     out=acc[:],
-                    lhsT=xc[:, sl].bitcast(FP8X4),
-                    lhsT_scale=xs[:, sl],
+                    lhsT=xc[:, cols].bitcast(FP8X4),
+                    lhsT_scale=xs[:, cols],
                     rhs=codes[:].bitcast(FP8X4),
                     rhs_scale=scales[:],
-                    start=(g == 0),
-                    stop=(g == PASSES - 1),
+                    start=(s == 0),
+                    stop=(s == PASSES - 1),
                 )
-            acc_ps[(m, c)] = acc
+            acc_ps[(g, c)] = acc
 
-        def cast_scalar(m, c):
-            part = slice((c % 2) * NT, (c % 2 + 1) * NT)
+        def cast_scalar(g, c):
             nc.scalar.activation(
-                out=f8_sb[(m, c // 2)][:, part], in_=o_sb[(m, c // 2)][:, part], func=COPY, scale=Y_SCALE, saturate=False
+                out=f8_sb[(g, c // 2)][:, in_half(c)], in_=o_sb[(g, c // 2)][:, in_half(c)], func=COPY, scale=Y_SCALE, saturate=False
             )
 
-        def cast_vector(m, c):
-            part = slice((c % 2) * NT, (c % 2 + 1) * NT)
+        def cast_vector(g, c):
             nc.vector.tensor_scalar(
-                out=f8_sb[(m, c // 2)][:, part],
-                in0=o_sb[(m, c // 2)][:, part],
+                out=f8_sb[(g, c // 2)][:, in_half(c)],
+                in0=o_sb[(g, c // 2)][:, in_half(c)],
                 scalar1=Y_SCALE,
                 scalar2=None,
                 op0=MULT,
                 saturate=False,
             )
 
-        def epilogue(m, c):
+        def epilogue(g, c):
             half = c // 2
             if c % 2 == 0:
-                o_sb[(m, half)] = o_pool.tile([P, HALF], F32, name="o", tag="o")
-                f8_sb[(m, half)] = f8_pool.tile([P, HALF], FP8, name="f8", tag="f8")
-            o = o_sb[(m, half)]
-            part = slice((c % 2) * NT, (c % 2 + 1) * NT)
-            nc.vector.tensor_tensor(out=o[:, part], in0=acc_ps[(m, c)][:], in1=lo_sb[(m, c)][:], op=ADD)
+                o_sb[(g, half)] = o_pool.tile([P, HALF], F32, name="o", tag="o")
+                f8_sb[(g, half)] = f8_pool.tile([P, HALF], FP8, name="f8", tag="f8")
+            o = o_sb[(g, half)]
+            nc.vector.tensor_tensor(out=o[:, in_half(c)], in0=acc_ps[(g, c)][:], in1=lo_sb[(g, c)][:], op=ADD)
             if c == CHUNKS - 1:
-                cast_scalar(m, c - 1)
-                cast_vector(m, c)
+                cast_scalar(g, c - 1)
+                cast_vector(g, c)
             elif c != CHUNKS - 2:
-                cast_scalar(m, c)
-            rows = slice(m * P, (m + 1) * P)
+                cast_scalar(g, c)
+            rows = slice(g * P, (g + 1) * P)
             wide = slice(half * HALF, (half + 1) * HALF)
             if half == 1:
-                nc.sync.dma_start(out=out_0[rows, c * NT:(c + 1) * NT], in_=o[:, part])
+                nc.sync.dma_start(out=out_0[rows, c * NT:(c + 1) * NT], in_=o[:, in_half(c)])
             elif c % 2 == 1:
                 nc.sync.dma_start(out=out_0[rows, wide], in_=o[:])
             if c % 2 == 1:
-                nc.sync.dma_start(out=out_1[rows, wide], in_=f8_sb[(m, half)][:].bitcast(U8))
+                nc.sync.dma_start(out=out_1[rows, wide], in_=f8_sb[(g, half)][:].bitcast(U8))
 
         load_x(0)
         load_x(1)
@@ -228,10 +228,10 @@ def tile_lorasequential_pa_kernel(tc, x, h_lora, lora_B, M, out_0, out_1):
         load_b(0, 4, 6)
         load_x(7)
         load_b(0, 6, 8)
-        for g in range(PASSES):
-            load_m(1, g)
-        for g in range(PASSES):
-            load_m_wide(1, g)
+        for s in range(PASSES):
+            load_m(1, s)
+        for s in range(PASSES):
+            load_m_wide(1, s)
         new_b(1)
         load_b(1, 0, 4)
         load_b(1, 4, 8)
@@ -250,15 +250,17 @@ def tile_lorasequential_pa_kernel(tc, x, h_lora, lora_B, M, out_0, out_1):
         unit_copy(0, 3)
         unit_quant(0, 3)
 
+        lora(0, 0)
         for c in range(CHUNKS):
-            for m in range(SEGS):
-                if c == 0 and m + X_AHEAD < SEGS:
-                    prep_x(m + X_AHEAD)
-                lora(m, c)
-                mx(m, c)
+            for g in range(SEGS):
+                if c == 0 and g + X_AHEAD < SEGS:
+                    prep_x(g + X_AHEAD)
+                if c * SEGS + g + 1 < CHUNKS * SEGS:
+                    lora((g + 1) % SEGS, c + (g + 1) // SEGS)
+                mx(g, c)
                 if c + 1 < CHUNKS:
-                    if m % 2 == 0:
-                        unit_copy(c + 1, m // 2)
+                    if g % 2 == 0:
+                        unit_copy(c + 1, g // 2)
                     else:
-                        unit_quant(c + 1, m // 2)
-                epilogue(m, c)
+                        unit_quant(c + 1, g // 2)
+                epilogue(g, c)

@@ -64,6 +64,7 @@ def tile_lorasequential_pa_kernel(tc, x, h_lora, lora_B, M, out_0, out_1):
         hT = keep.tile([P, SEGS * P], BF16, name="hT", tag="hT")
 
         xraw = {}
+        xgrp = {}
         mraw = {}
         btile = {}
         mgrp = {}
@@ -107,7 +108,7 @@ def tile_lorasequential_pa_kernel(tc, x, h_lora, lora_B, M, out_0, out_1):
         def load_h():
             nc.sync.dma_start(out=h_sb[:], in_=h_lora.rearrange("g b r -> (g b) r").rearrange("(p a) r -> p a r", a=SEGS))
 
-        def prep_x(g):
+        def turn_x(g):
             words = xraw[g][:].bitcast(F32)
             grp = xgrp_pool.tile([P, PASSES * P * PACK], BF16, name="xgrp", tag="xgrp", align_bytes=64)
             grp_words = grp[:].bitcast(F32).rearrange("p (s b u) -> p s b u", s=PASSES, u=2)
@@ -117,14 +118,21 @@ def tile_lorasequential_pa_kernel(tc, x, h_lora, lora_B, M, out_0, out_1):
                     for u in range(2):
                         nc.tensor.transpose(tp[:, s % 2, u, :], words[:, WORDS * s + u:WORDS * (s + 1):2], ident_f[:])
                 nc.scalar.copy(out=grp_words[:, 2 * bank:2 * bank + 2, :, :], in_=tp[:].rearrange("p s u b -> p s b u"))
+            xgrp[g] = grp
+
+        def quant_x(g):
             cols = slice(g * PASSES * P, (g + 1) * PASSES * P)
-            nc.vector.quantize_mx(out=xc[:, cols].bitcast(FP8X4), scales=xs[:, cols], in_=grp[:])
+            nc.vector.quantize_mx(out=xc[:, cols].bitcast(FP8X4), scales=xs[:, cols], in_=xgrp[g][:])
+
+        def prep_x(g):
+            turn_x(g)
+            quant_x(g)
 
         def prep_h():
             tp = ps_tp.tile([P, SEGS, P], BF16, name="tp", tag="tp")
             for a in range(SEGS):
                 nc.tensor.transpose(tp[:, a, :], h_sb[:, a, :], ident_b[:])
-            nc.vector.tensor_copy(out=hT[:].rearrange("r (p a) -> r p a", a=SEGS), in_=tp[:].rearrange("r a p -> r p a"))
+            nc.scalar.copy(out=hT[:].rearrange("r (p a) -> r p a", a=SEGS), in_=tp[:].rearrange("r a p -> r p a"))
 
         def unit_copy(c, s):
             raw = mraw[(c, s)]
@@ -158,21 +166,24 @@ def tile_lorasequential_pa_kernel(tc, x, h_lora, lora_B, M, out_0, out_1):
             nc.scalar.activation(out=lo[:], in_=lp[:], func=COPY, scale=LORA_GAIN)
             lo_sb[(g, c)] = lo
 
+        def mx_pass(g, c, s):
+            if s == 0:
+                acc_ps[(g, c)] = ps_mx.tile([P, NT], F32, name="acc", tag="acc")
+            codes, scales = mq[(c, s)]
+            cols = slice((g * PASSES + s) * P, (g * PASSES + s + 1) * P)
+            nc.tensor.matmul_mx(
+                out=acc_ps[(g, c)][:],
+                lhsT=xc[:, cols].bitcast(FP8X4),
+                lhsT_scale=xs[:, cols],
+                rhs=codes[:].bitcast(FP8X4),
+                rhs_scale=scales[:],
+                start=(s == 0),
+                stop=(s == PASSES - 1),
+            )
+
         def mx(g, c):
-            acc = ps_mx.tile([P, NT], F32, name="acc", tag="acc")
             for s in range(PASSES):
-                codes, scales = mq[(c, s)]
-                cols = slice((g * PASSES + s) * P, (g * PASSES + s + 1) * P)
-                nc.tensor.matmul_mx(
-                    out=acc[:],
-                    lhsT=xc[:, cols].bitcast(FP8X4),
-                    lhsT_scale=xs[:, cols],
-                    rhs=codes[:].bitcast(FP8X4),
-                    rhs_scale=scales[:],
-                    start=(s == 0),
-                    stop=(s == PASSES - 1),
-                )
-            acc_ps[(g, c)] = acc
+                mx_pass(g, c, s)
 
         def cast_scalar(g, c):
             nc.scalar.activation(
@@ -236,19 +247,33 @@ def tile_lorasequential_pa_kernel(tc, x, h_lora, lora_B, M, out_0, out_1):
         load_b(1, 0, 4)
         load_b(1, 4, 8)
 
-        prep_x(0)
-        prep_x(1)
-        unit_copy(0, 0)
-        prep_x(2)
-        unit_quant(0, 0)
-        unit_copy(0, 1)
-        prep_x(3)
-        unit_quant(0, 1)
-        unit_copy(0, 2)
-        prep_h()
-        unit_quant(0, 2)
-        unit_copy(0, 3)
-        unit_quant(0, 3)
+        with tc.manual_schedule():
+            turn_x(0)
+            turn_x(1)
+            quant_x(0)
+            unit_copy(0, 0)
+            quant_x(1)
+            turn_x(2)
+            unit_quant(0, 0)
+            mx_pass(0, 0, 0)
+            mx_pass(1, 0, 0)
+            unit_copy(0, 1)
+            quant_x(2)
+            turn_x(3)
+            unit_quant(0, 1)
+            mx_pass(2, 0, 0)
+            for g in range(3):
+                mx_pass(g, 0, 1)
+            unit_copy(0, 2)
+            quant_x(3)
+            prep_h()
+            unit_quant(0, 2)
+            mx_pass(3, 0, 0)
+            mx_pass(3, 0, 1)
+            for g in range(X_AHEAD):
+                mx_pass(g, 0, 2)
+            unit_copy(0, 3)
+            unit_quant(0, 3)
 
         lora(0, 0)
         for c in range(CHUNKS):
@@ -257,7 +282,10 @@ def tile_lorasequential_pa_kernel(tc, x, h_lora, lora_B, M, out_0, out_1):
                     prep_x(g + X_AHEAD)
                 if c * SEGS + g + 1 < CHUNKS * SEGS:
                     lora((g + 1) % SEGS, c + (g + 1) // SEGS)
-                mx(g, c)
+                if c == 0 and g < X_AHEAD:
+                    mx_pass(g, c, PASSES - 1)
+                else:
+                    mx(g, c)
                 if c + 1 < CHUNKS:
                     if g % 2 == 0:
                         unit_copy(c + 1, g // 2)

@@ -27,7 +27,7 @@ CHUNKS = N // NT
 LORA_GAIN = 2.0
 Y_SCALE = 150.0
 
-S_COLS = 128
+S_COLS = 64
 RUN = 8
 X_AHEAD = 4
 

@@ -30,6 +30,7 @@ Y_SCALE = 150.0
 S_COLS = 64
 RUN = 8
 X_AHEAD = 4
+TAIL_PARTS = 2
 
 
 def tile_lorasequential_pa_kernel(tc, x, h_lora, lora_B, M, out_0, out_1):
@@ -221,6 +222,41 @@ def tile_lorasequential_pa_kernel(tc, x, h_lora, lora_B, M, out_0, out_1):
             if c % 2 == 1:
                 nc.sync.dma_start(out=out_1[rows, wide], in_=f8_sb[(g, half)][:].bitcast(U8))
 
+        def last_tile(g, c):
+            half = c // 2
+            o = o_sb[(g, half)]
+            f8 = f8_sb[(g, half)]
+            width = NT // TAIL_PARTS
+            rows = slice(g * P, (g + 1) * P)
+            cast_scalar(g, c - 1)
+            for j in range(TAIL_PARTS):
+                acc = ps_mx.tile([P, width], F32, name="acc", tag="acc")
+                w = slice(j * width, (j + 1) * width)
+                for s in range(PASSES):
+                    codes, scales = mq[(c, s)]
+                    cols = slice((g * PASSES + s) * P, (g * PASSES + s + 1) * P)
+                    nc.tensor.matmul_mx(
+                        out=acc[:],
+                        lhsT=xc[:, cols].bitcast(FP8X4),
+                        lhsT_scale=xs[:, cols],
+                        rhs=codes[:, w].bitcast(FP8X4),
+                        rhs_scale=scales[:, w],
+                        start=(s == 0),
+                        stop=(s == PASSES - 1),
+                    )
+                first = NT + j * width
+                piece = slice(first, first + width)
+                nc.vector.tensor_tensor(out=o[:, piece], in0=acc[:], in1=lo_sb[(g, c)][:, w], op=ADD)
+                nc.sync.dma_start(out=out_0[rows, half * HALF + first:half * HALF + first + width], in_=o[:, piece])
+                if j + 1 < TAIL_PARTS:
+                    nc.scalar.activation(out=f8[:, piece], in_=o[:, piece], func=COPY, scale=Y_SCALE, saturate=False)
+                else:
+                    nc.vector.tensor_scalar(out=f8[:, piece], in0=o[:, piece], scalar1=Y_SCALE, scalar2=None, op0=MULT, saturate=False)
+                start_col = 0 if j == 0 else first
+                nc.sync.dma_start(
+                    out=out_1[rows, half * HALF + start_col:half * HALF + first + width], in_=f8[:, start_col:first + width].bitcast(U8)
+                )
+
         load_x(0)
         load_x(1)
         load_m(0, 0)
@@ -282,6 +318,9 @@ def tile_lorasequential_pa_kernel(tc, x, h_lora, lora_B, M, out_0, out_1):
                     prep_x(g + X_AHEAD)
                 if c * SEGS + g + 1 < CHUNKS * SEGS:
                     lora((g + 1) % SEGS, c + (g + 1) // SEGS)
+                if c == CHUNKS - 1 and g == SEGS - 1:
+                    last_tile(g, c)
+                    break
                 if c == 0 and g < X_AHEAD:
                     mx_pass(g, c, PASSES - 1)
                 else:

@@ -28,6 +28,7 @@ LORA_GAIN = 2.0
 Y_SCALE = 150.0
 
 S_COLS = 64
+S_COLS_EARLY = 160
 RUN = 8
 X_AHEAD = 4
 TAIL_PARTS = 2
@@ -138,7 +139,7 @@ def tile_lorasequential_pa_kernel(tc, x, h_lora, lora_B, M, out_0, out_1):
         def unit_copy(c, s):
             raw = mraw[(c, s)]
             grp = mgrp_pool.tile([P, NT, PACK], BF16, name="mgrp", tag="mgrp", align_bytes=64)
-            v_cols = NT - S_COLS
+            v_cols = NT - (S_COLS_EARLY if c < 2 else S_COLS)
             nc.vector.tensor_copy(
                 out=grp[:, 0:v_cols, :].rearrange("p (n i) t -> p n t i", i=RUN),
                 in_=raw[:, :, 0:v_cols].rearrange("p t (n i) -> p n t i", i=RUN),
@@ -186,12 +187,19 @@ def tile_lorasequential_pa_kernel(tc, x, h_lora, lora_B, M, out_0, out_1):
             for s in range(PASSES):
                 mx_pass(g, c, s)
 
+        def f8_tile(g, half):
+            if (g, half) not in f8_sb:
+                f8_sb[(g, half)] = f8_pool.tile([P, HALF], FP8, name="f8", tag="f8")
+            return f8_sb[(g, half)]
+
         def cast_scalar(g, c):
+            f8_tile(g, c // 2)
             nc.scalar.activation(
                 out=f8_sb[(g, c // 2)][:, in_half(c)], in_=o_sb[(g, c // 2)][:, in_half(c)], func=COPY, scale=Y_SCALE, saturate=False
             )
 
         def cast_vector(g, c):
+            f8_tile(g, c // 2)
             nc.vector.tensor_scalar(
                 out=f8_sb[(g, c // 2)][:, in_half(c)],
                 in0=o_sb[(g, c // 2)][:, in_half(c)],
@@ -204,14 +212,18 @@ def tile_lorasequential_pa_kernel(tc, x, h_lora, lora_B, M, out_0, out_1):
         def epilogue(g, c):
             half = c // 2
             if c % 2 == 0:
-                o_sb[(g, half)] = o_pool.tile([P, HALF], F32, name="o", tag="o")
-                f8_sb[(g, half)] = f8_pool.tile([P, HALF], FP8, name="f8", tag="f8")
+                if half == 0:
+                    o_sb[(g, half)] = o_pool.tile([P, HALF], F32, name="o", tag="o")
+                else:
+                    o_sb[(g, half)] = mraw_pool.tile([P, HALF], F32, name="mraw", tag="mraw")
             o = o_sb[(g, half)]
             nc.vector.tensor_tensor(out=o[:, in_half(c)], in0=acc_ps[(g, c)][:], in1=lo_sb[(g, c)][:], op=ADD)
             if c == CHUNKS - 1:
                 cast_scalar(g, c - 1)
                 cast_vector(g, c)
-            elif c != CHUNKS - 2:
+            elif c == CHUNKS - 2:
+                cast_scalar(g, 0)
+            elif c == 1:
                 cast_scalar(g, c)
             rows = slice(g * P, (g + 1) * P)
             wide = slice(half * HALF, (half + 1) * HALF)
@@ -219,13 +231,15 @@ def tile_lorasequential_pa_kernel(tc, x, h_lora, lora_B, M, out_0, out_1):
                 nc.sync.dma_start(out=out_0[rows, c * NT:(c + 1) * NT], in_=o[:, in_half(c)])
             elif c % 2 == 1:
                 nc.sync.dma_start(out=out_0[rows, wide], in_=o[:])
-            if c % 2 == 1:
+            if c == CHUNKS - 2:
+                nc.sync.dma_start(out=out_1[rows, 0:HALF], in_=f8_sb[(g, 0)][:].bitcast(U8))
+            if c == CHUNKS - 1:
                 nc.sync.dma_start(out=out_1[rows, wide], in_=f8_sb[(g, half)][:].bitcast(U8))
 
         def last_tile(g, c):
             half = c // 2
             o = o_sb[(g, half)]
-            f8 = f8_sb[(g, half)]
+            f8 = f8_tile(g, half)
             width = NT // TAIL_PARTS
             rows = slice(g * P, (g + 1) * P)
             cast_scalar(g, c - 1)

@@ -285,16 +285,20 @@ def tile_lorasequential_pa_kernel(tc, x, h_lora, lora_B, M, out_0, out_1):
         load_x(4)
         load_b(0, 2, 4)
         load_x(5)
+        load_m(1, 0)
         load_x(6)
         load_b(0, 4, 6)
+        load_m(1, 1)
         load_x(7)
+        load_m(1, 2)
         load_b(0, 6, 8)
-        for s in range(PASSES):
-            load_m(1, s)
-        for s in range(PASSES):
-            load_m_wide(1, s)
+        load_m(1, 3)
         new_b(1)
-        load_b(1, 0, 4)
+        for s in range(PASSES - 1):
+            load_m_wide(1, s)
+        load_b(1, 0, 2)
+        load_m_wide(1, PASSES - 1)
+        load_b(1, 2, 4)
         load_b(1, 4, 8)
 
         with tc.manual_schedule():

@@ -283,14 +283,14 @@ def tile_lorasequential_pa_kernel(tc, x, h_lora, lora_B, M, out_0, out_1):
         new_b(0)
         load_b(0, 0, 2)
         load_x(4)
+        load_m(1, 0)
         load_b(0, 2, 4)
         load_x(5)
-        load_m(1, 0)
+        load_m(1, 1)
         load_x(6)
         load_b(0, 4, 6)
-        load_m(1, 1)
-        load_x(7)
         load_m(1, 2)
+        load_x(7)
         load_b(0, 6, 8)
         load_m(1, 3)
         new_b(1)

from contextlib import ExitStack

import concourse.mybir as mybir
from concourse.masks import make_identity

ROWS, K, N, RANK, SEGS = 1024, 2048, 2048, 128, 8
FLOPS = 2 * ROWS * K * N + 2 * ROWS * RANK * N

F32 = mybir.dt.float32
BF16 = mybir.dt.bfloat16
U32 = mybir.dt.uint32
U8 = mybir.dt.uint8
FP8X4 = mybir.dt.float8_e4m3fn_x4
FP8 = mybir.dt.float8_e4m3fn
COPY = mybir.ActivationFunctionType.Copy
ADD = mybir.AluOpType.add
MULT = mybir.AluOpType.mult

P = 128
PACK = 4
K_PASS = P * PACK
PASSES = K // K_PASS
WORDS = K_PASS // 2
NT = 512
HALF = 2 * NT
CHUNKS = N // NT
LORA_GAIN = 2.0
Y_SCALE = 150.0

S_COLS = 64
S_COLS_EARLY = 160
RUN = 8
X_AHEAD = 4
TAIL_PARTS = 2


def tile_lorasequential_pa_kernel(tc, x, h_lora, lora_B, M, out_0, out_1):
    nc = tc.nc
    with ExitStack() as ctx:
        keep = ctx.enter_context(tc.tile_pool(name="keep", bufs=1))
        xraw_pool = ctx.enter_context(tc.tile_pool(name="xraw", bufs=X_AHEAD))
        xgrp_pool = ctx.enter_context(tc.tile_pool(name="xgrp", bufs=2))
        mraw_pool = ctx.enter_context(tc.tile_pool(name="mraw", bufs=2 * PASSES))
        mwide_pool = ctx.enter_context(tc.tile_pool(name="mwide", bufs=PASSES))
        mgrp_pool = ctx.enter_context(tc.tile_pool(name="mgrp", bufs=3))
        mq_pool = ctx.enter_context(tc.tile_pool(name="mq", bufs=2 * PASSES + 2))
        b_pool = ctx.enter_context(tc.tile_pool(name="bpool", bufs=2))
        lo_pool = ctx.enter_context(tc.tile_pool(name="lo", bufs=4))
        o_pool = ctx.enter_context(tc.tile_pool(name="o", bufs=SEGS))
        f8_pool = ctx.enter_context(tc.tile_pool(name="f8", bufs=SEGS))
        ps_mx = ctx.enter_context(tc.psum_pool(name="psmx", bufs=4))
        ps_lo = ctx.enter_context(tc.psum_pool(name="pslo", bufs=2))
        ps_tp = ctx.enter_context(tc.psum_pool(name="pstp", bufs=2))

        ident_f = keep.tile([P, P], F32, name="ident_f", tag="ident_f")
        make_identity(nc, ident_f[:])
        ident_b = keep.tile([P, P], BF16, name="ident_b", tag="ident_b")
        make_identity(nc, ident_b[:])
        warm = keep.tile([P, 2], F32, name="warm", tag="warm")
        nc.vector.memset(warm[:], 0.0)
        nc.scalar.activation(out=warm[:, 1:2], in_=warm[:, 0:1], func=COPY, scale=1.0)

        xc = keep.tile([P, SEGS * PASSES * P], U32, name="xc", tag="xc", align_bytes=64)
        xs = keep.tile([P, SEGS * PASSES * P], U8, name="xs", tag="xs", align_bytes=64)
        h_sb = keep.tile([P, SEGS, RANK], BF16, name="h_sb", tag="h_sb")
        hT = keep.tile([P, SEGS * P], BF16, name="hT", tag="hT")

        xraw = {}
        xgrp = {}
        mraw = {}
        btile = {}
        mgrp = {}
        mq = {}
        lo_sb = {}
        acc_ps = {}
        o_sb = {}
        f8_sb = {}

        def load_x(g):
            tile_x = xraw_pool.tile([P, K], BF16, name="xraw", tag="xraw")
            nc.sync.dma_start(out=tile_x[:], in_=x[g * P:(g + 1) * P, :])
            xraw[g] = tile_x

        def load_m(c, s):
            tile_m = mraw_pool.tile([P, PACK, NT], BF16, name="mraw", tag="mraw")
            nc.sync.dma_start(
                out=tile_m[:],
                in_=M[s * K_PASS:(s + 1) * K_PASS, c * NT:(c + 1) * NT].rearrange("(p t) w -> p t w", t=PACK),
            )
            mraw[(c, s)] = tile_m[:]

        def load_m_wide(half, s):
            tile_m = mwide_pool.tile([P, PACK, HALF], BF16, name="mwide", tag="mwide")
            nc.sync.dma_start(
                out=tile_m[:],
                in_=M[s * K_PASS:(s + 1) * K_PASS, half * HALF:(half + 1) * HALF].rearrange("(p t) w -> p t w", t=PACK),
            )
            mraw[(2 * half, s)] = tile_m[:, :, 0:NT]
            mraw[(2 * half + 1, s)] = tile_m[:, :, NT:HALF]

        def new_b(half):
            btile[half] = b_pool.tile([P, SEGS, HALF], BF16, name="btile", tag="btile")

        def load_b(half, g0, g1):
            nc.sync.dma_start(
                out=btile[half][:, g0:g1, :],
                in_=lora_B[g0:g1, :, half * HALF:(half + 1) * HALF].rearrange("g r w -> r g w"),
            )

        def load_h():
            nc.sync.dma_start(out=h_sb[:], in_=h_lora.rearrange("g b r -> (g b) r").rearrange("(p a) r -> p a r", a=SEGS))

        def turn_x(g):
            words = xraw[g][:].bitcast(F32)
            grp = xgrp_pool.tile([P, PASSES * P * PACK], BF16, name="xgrp", tag="xgrp", align_bytes=64)
            grp_words = grp[:].bitcast(F32).rearrange("p (s b u) -> p s b u", s=PASSES, u=2)
            for bank in range(PASSES // 2):
                tp = ps_tp.tile([P, 2, 2, P], F32, name="tp", tag="tp")
                for s in (2 * bank, 2 * bank + 1):
                    for u in range(2):
                        nc.tensor.transpose(tp[:, s % 2, u, :], words[:, WORDS * s + u:WORDS * (s + 1):2], ident_f[:])
                nc.scalar.copy(out=grp_words[:, 2 * bank:2 * bank + 2, :, :], in_=tp[:].rearrange("p s u b -> p s b u"))
            xgrp[g] = grp

        def quant_x(g):
            cols = slice(g * PASSES * P, (g + 1) * PASSES * P)
            nc.vector.quantize_mx(out=xc[:, cols].bitcast(FP8X4), scales=xs[:, cols], in_=xgrp[g][:])

        def prep_x(g):
            turn_x(g)
            quant_x(g)

        def prep_h():
            tp = ps_tp.tile([P, SEGS, P], BF16, name="tp", tag="tp")
            for a in range(SEGS):
                nc.tensor.transpose(tp[:, a, :], h_sb[:, a, :], ident_b[:])
            nc.scalar.copy(out=hT[:].rearrange("r (p a) -> r p a", a=SEGS), in_=tp[:].rearrange("r a p -> r p a"))

        def unit_copy(c, s):
            raw = mraw[(c, s)]
            grp = mgrp_pool.tile([P, NT, PACK], BF16, name="mgrp", tag="mgrp", align_bytes=64)
            v_cols = NT - (S_COLS_EARLY if c < 2 else S_COLS)
            nc.vector.tensor_copy(
                out=grp[:, 0:v_cols, :].rearrange("p (n i) t -> p n t i", i=RUN),
                in_=raw[:, :, 0:v_cols].rearrange("p t (n i) -> p n t i", i=RUN),
            )
            nc.scalar.copy(
                out=grp[:, v_cols:NT, :].rearrange("p (n i) t -> p n t i", i=RUN),
                in_=raw[:, :, v_cols:NT].rearrange("p t (n i) -> p n t i", i=RUN),
            )
            mgrp[(c, s)] = grp

        def unit_quant(c, s):
            codes = mq_pool.tile([P, NT], U32, name="mcodes", tag="mcodes", align_bytes=64)
            scales = mq_pool.tile([P, NT], U8, name="mscales", tag="mscales", align_bytes=64)
            nc.vector.quantize_mx(
                out=codes[:].bitcast(FP8X4), scales=scales[:], in_=mgrp[(c, s)][:].rearrange("p w t -> p (w t)")
            )
            mq[(c, s)] = (codes, scales)

        def in_half(c):
            return slice((c % 2) * NT, (c % 2 + 1) * NT)

        def lora(g, c):
            lp = ps_lo.tile([P, NT], F32, name="lp", tag="lp")
            nc.tensor.matmul(out=lp[:], lhsT=hT[:, g * P:(g + 1) * P], rhs=btile[c // 2][:, g, in_half(c)], start=True, stop=True)
            lo = lo_pool.tile([P, NT], F32, name="lo", tag="lo")
            nc.scalar.activation(out=lo[:], in_=lp[:], func=COPY, scale=LORA_GAIN)
            lo_sb[(g, c)] = lo

        def mx_pass(g, c, s):
            if s == 0:
                acc_ps[(g, c)] = ps_mx.tile([P, NT], F32, name="acc", tag="acc")
            codes, scales = mq[(c, s)]
            cols = slice((g * PASSES + s) * P, (g * PASSES + s + 1) * P)
            nc.tensor.matmul_mx(
                out=acc_ps[(g, c)][:],
                lhsT=xc[:, cols].bitcast(FP8X4),
                lhsT_scale=xs[:, cols],
                rhs=codes[:].bitcast(FP8X4),
                rhs_scale=scales[:],
                start=(s == 0),
                stop=(s == PASSES - 1),
            )

        def mx(g, c):
            for s in range(PASSES):
                mx_pass(g, c, s)

        def f8_tile(g, half):
            if (g, half) not in f8_sb:
                f8_sb[(g, half)] = f8_pool.tile([P, HALF], FP8, name="f8", tag="f8")
            return f8_sb[(g, half)]

        def cast_scalar(g, c):
            f8_tile(g, c // 2)
            nc.scalar.activation(
                out=f8_sb[(g, c // 2)][:, in_half(c)], in_=o_sb[(g, c // 2)][:, in_half(c)], func=COPY, scale=Y_SCALE, saturate=False
            )

        def cast_vector(g, c):
            f8_tile(g, c // 2)
            nc.vector.tensor_scalar(
                out=f8_sb[(g, c // 2)][:, in_half(c)],
                in0=o_sb[(g, c // 2)][:, in_half(c)],
                scalar1=Y_SCALE,
                scalar2=None,
                op0=MULT,
                saturate=False,
            )

        def epilogue(g, c):
            half = c // 2
            if c % 2 == 0:
                if half == 0:
                    o_sb[(g, half)] = o_pool.tile([P, HALF], F32, name="o", tag="o")
                else:
                    o_sb[(g, half)] = mraw_pool.tile([P, HALF], F32, name="mraw", tag="mraw")
            o = o_sb[(g, half)]
            nc.vector.tensor_tensor(out=o[:, in_half(c)], in0=acc_ps[(g, c)][:], in1=lo_sb[(g, c)][:], op=ADD)
            if c == CHUNKS - 1:
                cast_scalar(g, c - 1)
                cast_vector(g, c)
            elif c == CHUNKS - 2:
                cast_scalar(g, 0)
            elif c == 1:
                cast_scalar(g, c)
            rows = slice(g * P, (g + 1) * P)
            wide = slice(half * HALF, (half + 1) * HALF)
            if half == 1:
                nc.sync.dma_start(out=out_0[rows, c * NT:(c + 1) * NT], in_=o[:, in_half(c)])
            elif c % 2 == 1:
                nc.sync.dma_start(out=out_0[rows, wide], in_=o[:])
            if c == CHUNKS - 2:
                nc.sync.dma_start(out=out_1[rows, 0:HALF], in_=f8_sb[(g, 0)][:].bitcast(U8))
            if c == CHUNKS - 1:
                nc.sync.dma_start(out=out_1[rows, wide], in_=f8_sb[(g, half)][:].bitcast(U8))

        def last_tile(g, c):
            half = c // 2
            o = o_sb[(g, half)]
            f8 = f8_tile(g, half)
            width = NT // TAIL_PARTS
            rows = slice(g * P, (g + 1) * P)
            cast_scalar(g, c - 1)
            for j in range(TAIL_PARTS):
                acc = ps_mx.tile([P, width], F32, name="acc", tag="acc")
                w = slice(j * width, (j + 1) * width)
                for s in range(PASSES):
                    codes, scales = mq[(c, s)]
                    cols = slice((g * PASSES + s) * P, (g * PASSES + s + 1) * P)
                    nc.tensor.matmul_mx(
                        out=acc[:],
                        lhsT=xc[:, cols].bitcast(FP8X4),
                        lhsT_scale=xs[:, cols],
                        rhs=codes[:, w].bitcast(FP8X4),
                        rhs_scale=scales[:, w],
                        start=(s == 0),
                        stop=(s == PASSES - 1),
                    )
                first = NT + j * width
                piece = slice(first, first + width)
                nc.vector.tensor_tensor(out=o[:, piece], in0=acc[:], in1=lo_sb[(g, c)][:, w], op=ADD)
                nc.sync.dma_start(out=out_0[rows, half * HALF + first:half * HALF + first + width], in_=o[:, piece])
                if j + 1 < TAIL_PARTS:
                    nc.scalar.activation(out=f8[:, piece], in_=o[:, piece], func=COPY, scale=Y_SCALE, saturate=False)
                else:
                    nc.vector.tensor_scalar(out=f8[:, piece], in0=o[:, piece], scalar1=Y_SCALE, scalar2=None, op0=MULT, saturate=False)
                start_col = 0 if j == 0 else first
                nc.sync.dma_start(
                    out=out_1[rows, half * HALF + start_col:half * HALF + first + width], in_=f8[:, start_col:first + width].bitcast(U8)
                )

        load_x(0)
        load_x(1)
        load_m(0, 0)
        load_x(2)
        load_m(0, 1)
        load_x(3)
        load_m(0, 2)
        load_h()
        load_m(0, 3)
        new_b(0)
        load_b(0, 0, 2)
        load_x(4)
        load_m(1, 0)
        load_b(0, 2, 4)
        load_x(5)
        load_m(1, 1)
        load_x(6)
        load_b(0, 4, 6)
        load_m(1, 2)
        load_x(7)
        load_b(0, 6, 8)
        load_m(1, 3)
        new_b(1)
        for s in range(PASSES - 1):
            load_m_wide(1, s)
        load_b(1, 0, 2)
        load_m_wide(1, PASSES - 1)
        load_b(1, 2, 4)
        load_b(1, 4, 8)

        with tc.manual_schedule():
            turn_x(0)
            turn_x(1)
            quant_x(0)
            unit_copy(0, 0)
            quant_x(1)
            turn_x(2)
            unit_quant(0, 0)
            mx_pass(0, 0, 0)
            mx_pass(1, 0, 0)
            unit_copy(0, 1)
            quant_x(2)
            turn_x(3)
            unit_quant(0, 1)
            mx_pass(2, 0, 0)
            for g in range(3):
                mx_pass(g, 0, 1)
            unit_copy(0, 2)
            quant_x(3)
            prep_h()
            unit_quant(0, 2)
            mx_pass(3, 0, 0)
            mx_pass(3, 0, 1)
            for g in range(X_AHEAD):
                mx_pass(g, 0, 2)
            unit_copy(0, 3)
            unit_quant(0, 3)

        lora(0, 0)
        for c in range(CHUNKS):
            for g in range(SEGS):
                if c == 0 and g + X_AHEAD < SEGS:
                    prep_x(g + X_AHEAD)
                if c * SEGS + g + 1 < CHUNKS * SEGS:
                    lora((g + 1) % SEGS, c + (g + 1) // SEGS)
                if c == CHUNKS - 1 and g == SEGS - 1:
                    last_tile(g, c)
                    break
                if c == 0 and g < X_AHEAD:
                    mx_pass(g, c, PASSES - 1)
                else:
                    mx(g, c)
                if c + 1 < CHUNKS:
                    if g % 2 == 0:
                        unit_copy(c + 1, g // 2)
                    else:
                        unit_quant(c + 1, g // 2)
                epilogue(g, c)
